import numpy as np
import ml_dtypes


def mxq(x, axis, fmt="e4m3"):
    dtype, down = {"e4m3": (ml_dtypes.float8_e4m3fn, 7), "e5m2": (ml_dtypes.float8_e5m2, 14)}[fmt]
    v = np.moveaxis(np.asarray(x, np.float32).astype(ml_dtypes.bfloat16).astype(np.float64), axis, -1)
    blocks = v.reshape(v.shape[:-1] + (-1, 32))
    amax = np.abs(blocks).max(-1, keepdims=True)
    byte = np.maximum(np.where(amax > 0, np.frexp(amax)[1] - 1 + 127, 0) - down, 1)
    scale = np.exp2(byte - 127.0)
    codes = (blocks / scale).astype(np.float32).astype(dtype).astype(np.float64)
    return np.moveaxis((codes * scale).reshape(v.shape), -1, axis)


WIDE = False


def mx_kscale(k):
    if not WIDE:
        return np.ones(k)
    levels = np.array([18, -18])
    if k % 512:
        return np.exp2(np.random.permutation(np.resize(levels, k // 32))).repeat(32)
    a = np.empty((k // 512, 16))
    for p in range(k // 512):
        a[p, :8] = np.random.permutation(np.resize(levels, 8))
        for g in range(8):
            far = levels[np.abs(levels - a[p, g]) >= 10]
            a[p, g + 8] = far[np.random.randint(len(far))]
    return np.exp2(a.ravel()).repeat(32)


BF16 = ml_dtypes.bfloat16


def bf(x):
    return np.asarray(x, np.float32).astype(BF16)


def f64(x):
    return np.asarray(x).astype(np.float64)


B, N, D, H, S = 2, 512, 512, 1024, 128
T = B * N
QS = 2.3 / N ** 0.25


def silu(z):
    return z / (1.0 + np.exp(-z))


def setup_inputs():
    s = mx_kscale(T).reshape(B, N, 1)
    c = mx_kscale(D)
    q = bf(np.random.standard_normal((B, N, S)) * QS)
    k = bf(np.random.standard_normal((B, N, S)) * QS)
    u0 = bf(silu(0.7 * np.random.standard_normal((B, N, H))))
    v = bf(silu(0.7 * np.random.standard_normal((B, N, H))))
    w0 = bf(np.random.standard_normal((H, D)) / np.sqrt(H))
    b_o = bf(0.1 * np.random.standard_normal(D))
    g = bf(np.random.standard_normal((B, N, D)) * np.exp2(np.random.randint(-6, 1, (B, N, 1))) / s * c)
    qk = f64(q) @ f64(k).transpose(0, 2, 1) * (1.0 / np.sqrt(S))
    av = np.square(np.maximum(qk, 0.0)) @ f64(v)
    return {"q": q, "k": k, "u": bf(f64(u0) * s), "v": v, "W_o": bf(f64(w0) / c), "b_o": b_o,
            "av": np.asarray(av, np.float32), "grad_out": g}


def reference(q, k, u, v, W_o, b_o, av, grad_out):
    g = f64(grad_out).reshape(T, D)
    a = f64(av).reshape(T, H)
    gated = f64(u).reshape(T, H) * a
    dgated = mxq(g, 1, "e5m2") @ mxq(f64(W_o), 1, "e4m3").T
    du = (dgated * a).reshape(B, N, H)
    dW_o = mxq(gated, 0, "e4m3").T @ mxq(g, 0, "e5m2")
    return du, dW_o

@@ -1,0 +1,223 @@
+from contextlib import ExitStack
+
+import concourse.mybir as mybir
+from concourse.masks import make_identity
+
+F32 = mybir.dt.float32
+BF16 = mybir.dt.bfloat16
+U32 = mybir.dt.uint32
+U8 = mybir.dt.uint8
+E4M3 = mybir.dt.float8_e4m3fn_x4
+E5M2 = mybir.dt.float8_e5m2_x4
+MULT = mybir.AluOpType.mult
+
+B, N, D, H = 2, 512, 512, 1024
+P = 128
+PACK = 4
+HALF = 512
+RUN = 4
+
+FLOPS = 2 * 2 * B * N * D * H
+BYTES = B * N * H * (2 + 4 + 4) + B * N * D * 2 + H * D * (2 + 4)
+
+
+def tile_gatedattentionunit_pb_v_kernel(tc, q, k, u, v, W_o, b_o, av, grad_out, out_0, out_1):
+    nc = tc.nc
+
+    with ExitStack() as ctx:
+        sb = ctx.enter_context(tc.tile_pool(name="sb", bufs=1))
+        ps = ctx.enter_context(tc.psum_pool(name="ps", bufs=1))
+        ctx.enter_context(tc.manual_schedule())
+
+        def sbuf(name, shape, dtype):
+            return sb.tile(shape, dtype, name=name, align_bytes=64)
+
+        def bank(index):
+            return ps.tile([P, HALF], F32, name="bank%d" % index)
+
+        def by_slot(rows):
+            return rows.rearrange("(p j) w -> p j w", j=PACK)
+
+        g_raw = [sbuf("g_raw%d" % b, [P, PACK, D], BF16) for b in range(B)]
+        w_raw = [sbuf("w_raw%d" % h, [P, PACK, D], BF16) for h in range(2)]
+        u_raw = [sbuf("u_raw%d" % b, [P, PACK, H], BF16) for b in range(B)]
+        av_raw = [sbuf("av_raw%d" % b, [P, PACK, H], F32) for b in range(B)]
+
+        def load_av(b):
+            for s in range(2):
+                nc.sync.dma_start(out=av_raw[b][:, 2 * s : 2 * s + 2, :], in_=by_slot(av[b])[:, 2 * s : 2 * s + 2, :])
+
+        nc.sync.dma_start(out=g_raw[0][:], in_=by_slot(grad_out[0]))
+        for h in range(2):
+            nc.sync.dma_start(out=w_raw[h][:], in_=by_slot(W_o[h * HALF : (h + 1) * HALF, :]))
+        load_av(0)
+        nc.sync.dma_start(out=u_raw[0][:], in_=by_slot(u[0]))
+        nc.sync.dma_start(out=g_raw[1][:], in_=by_slot(grad_out[1]))
+        nc.sync.dma_start(out=u_raw[1][:], in_=by_slot(u[1]))
+        load_av(1)
+
+        ident = sbuf("ident", [P, P], F32)
+        make_identity(nc, ident[:])
+
+        def interleaved(tile):
+            return tile[:].rearrange("p (c i t) -> p c t i", i=RUN, t=PACK)
+
+        def slot_runs(view):
+            return view.rearrange("p t (c i) -> p c t i", i=RUN)
+
+        def quantize(name, grouped, fmt):
+            codes = sbuf(name + "_codes", [P, HALF], U32)
+            scales = sbuf(name + "_scales", [P, HALF], U8)
+            nc.vector.quantize_mx(out=codes[:].bitcast(fmt), scales=scales[:], in_=grouped[:])
+            return codes, scales, fmt
+
+        def interleave_g(b, copy):
+            grouped = sbuf("g_tok%d" % b, [P, D * PACK], BF16)
+            copy(out=interleaved(grouped), in_=slot_runs(g_raw[b][:]))
+            return grouped
+
+        def transpose(name, raw, first_bank, slot_major):
+            grouped = sbuf(name, [P, HALF * PACK], BF16)
+            words = raw[:].rearrange("p j d -> p (j d)").bitcast(F32)
+            dst = grouped[:].bitcast(F32)
+            for s in range(2):
+                xt = bank(first_bank + s)
+                for jj in range(2):
+                    for e in range(2):
+                        j = 2 * s + jj
+                        nc.tensor.transpose(
+                            xt[:, (2 * jj + e) * P : (2 * jj + e + 1) * P],
+                            words[:, 256 * j + e : 256 * (j + 1) : 2],
+                            ident[:],
+                        )
+                if slot_major:
+                    nc.scalar.copy(
+                        out=dst.rearrange("p (j r e) -> p j r e", j=PACK, e=2)[:, 2 * s : 2 * s + 2],
+                        in_=xt[:].rearrange("p (j e r) -> p j r e", j=2, e=2),
+                    )
+                else:
+                    nc.scalar.copy(
+                        out=dst.rearrange("p (r j e) -> p r j e", j=PACK, e=2)[:, :, 2 * s : 2 * s + 2, :],
+                        in_=xt[:].rearrange("p (j e r) -> p r j e", j=2, e=2),
+                    )
+            return grouped
+
+        def matmul(acc, stationary, block, moving, start, stop):
+            cols = slice(block * P, (block + 1) * P)
+            nc.tensor.matmul_mx(
+                out=acc[:],
+                lhsT=stationary[0][:, cols].bitcast(stationary[2]),
+                lhsT_scale=stationary[1][:, cols],
+                rhs=moving[0][:].bitcast(moving[2]),
+                rhs_scale=moving[1][:],
+                start=start,
+                stop=stop,
+            )
+
+        def gate(b, h):
+            cols = slice(h * HALF, (h + 1) * HALF)
+            grouped = sbuf("gated%d%d" % (b, h), [P, HALF * PACK], BF16)
+            nc.vector.tensor_tensor(
+                out=interleaved(grouped),
+                in0=slot_runs(u_raw[b][:, :, cols]),
+                in1=slot_runs(av_raw[b][:, :, cols]),
+                op=MULT,
+            )
+            return grouped
+
+        du = [sbuf("du%d" % b, [P, PACK, H], F32) for b in range(B)]
+        dw = [sbuf("dw%d" % h, [P, PACK, D], F32) for h in range(2)]
+        DU_BANK = 4
+
+        def du_products(g_feat, w_q, s):
+            accs = {}
+            for h in range(2):
+                for jj in range(2):
+                    acc = bank(DU_BANK + 2 * h + jj)
+                    matmul(acc, g_feat, 2 * s + jj, w_q[h], True, True)
+                    accs[(2 * s + jj, h)] = acc
+            return accs
+
+        def du_scale(b, j, h, accs):
+            cols = slice(h * HALF, (h + 1) * HALF)
+            nc.vector.tensor_tensor(out=du[b][:, j, cols], in0=accs[(j, h)][:], in1=av_raw[b][:, j, cols], op=MULT)
+
+        def du_store(b, j0, j1):
+            nc.sync.dma_start(out=by_slot(out_0[b])[:, j0:j1, :], in_=du[b][:, j0:j1, :])
+
+        def du_pair(b, s, accs):
+            for h in range(2):
+                for jj in range(2):
+                    du_scale(b, 2 * s + jj, h, accs)
+            du_store(b, 2 * s, 2 * s + 2)
+
+        def dw_open(gated_q, g_tok):
+            accs = [bank(m) for m in range(PACK)]
+            for m in range(PACK):
+                matmul(accs[m], gated_q, m, g_tok, True, False)
+            return accs
+
+        def dw_close(h, accs, gated_q, g_tok):
+            for m in range(PACK):
+                matmul(accs[m], gated_q, m, g_tok, False, True)
+                nc.scalar.copy(out=dw[h][:, m, :], in_=accs[m][:])
+
+        def dw_store(h):
+            rows = out_1[h * HALF : (h + 1) * HALF, :].rearrange("(m p) d -> p m d", p=P)
+            for s in range(2):
+                nc.sync.dma_start(out=rows[:, 2 * s : 2 * s + 2, :], in_=dw[h][:, 2 * s : 2 * s + 2, :])
+
+        g_tok0 = interleave_g(0, nc.vector.tensor_copy)
+        g_feat0 = transpose("g_feat0", g_raw[0], 0, True)
+        w_t0 = transpose("w_t0", w_raw[0], 2, False)
+        g_feat0_q = quantize("g_feat0", g_feat0, E5M2)
+        g_tok0_q = quantize("g_tok0", g_tok0, E5M2)
+        w_t1 = transpose("w_t1", w_raw[1], 0, False)
+        w_q = [quantize("w0", w_t0, E4M3), quantize("w1", w_t1, E4M3)]
+        for s in range(2):
+            du_pair(0, s, du_products(g_feat0_q, w_q, s))
+
+        g_feat1 = transpose("g_feat1", g_raw[1], 2, True)
+        g_tok1 = interleave_g(1, nc.scalar.copy)
+        gated0 = [gate(0, h) for h in range(2)]
+        g_feat1_q = quantize("g_feat1", g_feat1, E5M2)
+        gated0_q = [quantize("gated0%d" % h, gated0[h], E4M3) for h in range(2)]
+        g_tok1_q = quantize("g_tok1", g_tok1, E5M2)
+
+        accs = {}
+
+        def du_product(j, h):
+            acc = bank(DU_BANK + (2 * j + h) % 4)
+            matmul(acc, g_feat1_q, j, w_q[h], True, True)
+            accs[(j, h)] = acc
+
+        for j in range(2):
+            for h in range(2):
+                du_product(j, h)
+        dw_accs = dw_open(gated0_q[0], g_tok0_q)
+
+        gated10 = gate(1, 0)
+        du_scale(1, 0, 0, accs)
+        gated10_q = quantize("gated10", gated10, E4M3)
+        du_scale(1, 0, 1, accs)
+        du_store(1, 0, 1)
+        dw_close(0, dw_accs, gated10_q, g_tok1_q)
+        dw_store(0)
+        for h in range(2):
+            du_product(2, h)
+        dw_accs = dw_open(gated0_q[1], g_tok0_q)
+        gated11 = gate(1, 1)
+        du_scale(1, 1, 0, accs)
+        gated11_q = quantize("gated11", gated11, E4M3)
+        du_scale(1, 1, 1, accs)
+        du_store(1, 1, 2)
+        dw_close(1, dw_accs, gated11_q, g_tok1_q)
+        for h in range(2):
+            du_product(3, h)
+        for h in range(2):
+            du_scale(1, 2, h, accs)
+        du_store(1, 2, 3)
+        dw_store(1)
+        for h in range(2):
+            du_scale(1, 3, h, accs)
+        du_store(1, 3, 4)

@@ -38,68 +38,73 @@ def tile_gatedattentionunit_pb_v_kernel(tc, q, k, u, v, W_o, b_o, av, grad_out, 
         def by_slot(rows):
             return rows.rearrange("(p j) w -> p j w", j=PACK)
 
-        g_raw = [sbuf("g_raw%d" % b, [P, PACK, D], BF16) for b in range(B)]
-        w_raw = [sbuf("w_raw%d" % h, [P, PACK, D], BF16) for h in range(2)]
-        u_raw = [sbuf("u_raw%d" % b, [P, PACK, H], BF16) for b in range(B)]
-        av_raw = [sbuf("av_raw%d" % b, [P, PACK, H], F32) for b in range(B)]
+        def half(h):
+            return slice(h * HALF, (h + 1) * HALF)
 
-        def load_av(b):
+        def load(name, rows, dtype):
+            tile = sbuf(name, list(rows.shape), dtype)
+            nc.sync.dma_start(out=tile[:], in_=rows)
+            return tile
+
+        def load_pairs(name, rows, dtype):
+            tile = sbuf(name, list(rows.shape), dtype)
             for s in range(2):
-                nc.sync.dma_start(out=av_raw[b][:, 2 * s : 2 * s + 2, :], in_=by_slot(av[b])[:, 2 * s : 2 * s + 2, :])
+                nc.sync.dma_start(out=tile[:, 2 * s : 2 * s + 2, :], in_=rows[:, 2 * s : 2 * s + 2, :])
+            return tile
 
-        nc.sync.dma_start(out=g_raw[0][:], in_=by_slot(grad_out[0]))
-        for h in range(2):
-            nc.sync.dma_start(out=w_raw[h][:], in_=by_slot(W_o[h * HALF : (h + 1) * HALF, :]))
-        load_av(0)
-        nc.sync.dma_start(out=u_raw[0][:], in_=by_slot(u[0]))
-        nc.sync.dma_start(out=g_raw[1][:], in_=by_slot(grad_out[1]))
-        nc.sync.dma_start(out=u_raw[1][:], in_=by_slot(u[1]))
-        load_av(1)
-
-        ident = sbuf("ident", [P, P], F32)
-        make_identity(nc, ident[:])
-
-        def interleaved(tile):
-            return tile[:].rearrange("p (c i t) -> p c t i", i=RUN, t=PACK)
+        def interleaved(view):
+            return view.rearrange("p (c i t) -> p c t i", i=RUN, t=PACK)
 
         def slot_runs(view):
             return view.rearrange("p t (c i) -> p c t i", i=RUN)
 
-        def quantize(name, grouped, fmt):
-            codes = sbuf(name + "_codes", [P, HALF], U32)
-            scales = sbuf(name + "_scales", [P, HALF], U8)
-            nc.vector.quantize_mx(out=codes[:].bitcast(fmt), scales=scales[:], in_=grouped[:])
-            return codes, scales, fmt
+        def mx_operand(name, fmt):
+            return sbuf(name + "_codes", [P, HALF], U32), sbuf(name + "_scales", [P, HALF], U8), fmt
+
+        def quantize(operand, grouped, c0=0, c1=HALF):
+            codes, scales, fmt = operand
+            nc.vector.quantize_mx(
+                out=codes[:, c0:c1].bitcast(fmt), scales=scales[:, c0:c1], in_=grouped[:, PACK * c0 : PACK * c1]
+            )
 
         def interleave_g(b, copy):
             grouped = sbuf("g_tok%d" % b, [P, D * PACK], BF16)
-            copy(out=interleaved(grouped), in_=slot_runs(g_raw[b][:]))
+            copy(out=interleaved(grouped[:]), in_=slot_runs(g_raw[b][:]))
             return grouped
 
-        def transpose(name, raw, first_bank, slot_major):
-            grouped = sbuf(name, [P, HALF * PACK], BF16)
-            words = raw[:].rearrange("p j d -> p (j d)").bitcast(F32)
-            dst = grouped[:].bitcast(F32)
+        def transpose_pair(raw, s, bank_index):
+            xt = bank(bank_index)
+            for jj in range(2):
+                words = raw[:, 2 * s + jj, :].bitcast(F32)
+                for e in range(2):
+                    nc.tensor.transpose(xt[:, (2 * jj + e) * P : (2 * jj + e + 1) * P], words[:, e::2], ident[:])
+            return xt
+
+        def transpose_g(b, first_bank):
+            tiles = []
             for s in range(2):
-                xt = bank(first_bank + s)
-                for jj in range(2):
-                    for e in range(2):
-                        j = 2 * s + jj
-                        nc.tensor.transpose(
-                            xt[:, (2 * jj + e) * P : (2 * jj + e + 1) * P],
-                            words[:, 256 * j + e : 256 * (j + 1) : 2],
-                            ident[:],
-                        )
-                if slot_major:
-                    nc.scalar.copy(
-                        out=dst.rearrange("p (j r e) -> p j r e", j=PACK, e=2)[:, 2 * s : 2 * s + 2],
-                        in_=xt[:].rearrange("p (j e r) -> p j r e", j=2, e=2),
-                    )
-                else:
-                    nc.scalar.copy(
-                        out=dst.rearrange("p (r j e) -> p r j e", j=PACK, e=2)[:, :, 2 * s : 2 * s + 2, :],
-                        in_=xt[:].rearrange("p (j e r) -> p r j e", j=2, e=2),
-                    )
+                xt = transpose_pair(g_raw[b], s, first_bank + s)
+                grouped = sbuf("g_feat%d%d" % (b, s), [P, 2 * P * PACK], BF16)
+                nc.scalar.copy(
+                    out=grouped[:].bitcast(F32).rearrange("p (j r e) -> p j r e", j=2, e=2),
+                    in_=xt[:].rearrange("p (j e r) -> p j r e", j=2, e=2),
+                )
+                tiles.append(grouped)
+            return tiles
+
+        def quantize_pair(operand, grouped, s):
+            codes, scales, fmt = operand
+            cols = slice(2 * P * s, 2 * P * (s + 1))
+            nc.vector.quantize_mx(out=codes[:, cols].bitcast(fmt), scales=scales[:, cols], in_=grouped[s][:])
+
+        def transpose_w(h, first_bank):
+            grouped = sbuf("w_t%d" % h, [P, HALF * PACK], BF16)
+            for s in range(2):
+                xt = transpose_pair(w_raw[h], s, first_bank + s)
+                nc.scalar.copy(
+                    out=grouped[:].bitcast(F32).rearrange("p (r j e) -> p r j e", j=PACK, e=2)[:, :, 2 * s : 2 * s + 2, :],
+                    in_=xt[:].rearrange("p (j e r) -> p r j e", j=2, e=2),
+                )
             return grouped
 
         def matmul(acc, stationary, block, moving, start, stop):
@@ -114,110 +119,126 @@ def tile_gatedattentionunit_pb_v_kernel(tc, q, k, u, v, W_o, b_o, av, grad_out, 
                 stop=stop,
             )
 
-        def gate(b, h):
-            cols = slice(h * HALF, (h + 1) * HALF)
-            grouped = sbuf("gated%d%d" % (b, h), [P, HALF * PACK], BF16)
+        def gate(b, h, c0=0, c1=HALF):
             nc.vector.tensor_tensor(
-                out=interleaved(grouped),
-                in0=slot_runs(u_raw[b][:, :, cols]),
-                in1=slot_runs(av_raw[b][:, :, cols]),
+                out=interleaved(gated[b][h][:, PACK * c0 : PACK * c1]),
+                in0=slot_runs(u_raw[b][h][:, :, c0:c1]),
+                in1=slot_runs(av_raw[b][h][:, :, c0:c1]),
                 op=MULT,
             )
-            return grouped
 
-        du = [sbuf("du%d" % b, [P, PACK, H], F32) for b in range(B)]
-        dw = [sbuf("dw%d" % h, [P, PACK, D], F32) for h in range(2)]
         DU_BANK = 4
+        du_accs = {}
+        dw_accs = {}
 
-        def du_products(g_feat, w_q, s):
-            accs = {}
-            for h in range(2):
-                for jj in range(2):
-                    acc = bank(DU_BANK + 2 * h + jj)
-                    matmul(acc, g_feat, 2 * s + jj, w_q[h], True, True)
-                    accs[(2 * s + jj, h)] = acc
-            return accs
+        def du_product(b, h, j):
+            du_accs[j] = bank(DU_BANK + j)
+            matmul(du_accs[j], g_feat_q[b], j, w_q[h], True, True)
 
-        def du_scale(b, j, h, accs):
-            cols = slice(h * HALF, (h + 1) * HALF)
-            nc.vector.tensor_tensor(out=du[b][:, j, cols], in0=accs[(j, h)][:], in1=av_raw[b][:, j, cols], op=MULT)
+        def du_scale(b, h, j):
+            nc.vector.tensor_tensor(out=du[b][h][:, j, :], in0=du_accs[j][:], in1=av_raw[b][h][:, j, :], op=MULT)
 
-        def du_store(b, j0, j1):
-            nc.sync.dma_start(out=by_slot(out_0[b])[:, j0:j1, :], in_=du[b][:, j0:j1, :])
+        def du_store(b, h, j0=0, j1=PACK):
+            nc.sync.dma_start(out=by_slot(out_0[b])[:, j0:j1, half(h)], in_=du[b][h][:, j0:j1, :])
 
-        def du_pair(b, s, accs):
-            for h in range(2):
-                for jj in range(2):
-                    du_scale(b, 2 * s + jj, h, accs)
-            du_store(b, 2 * s, 2 * s + 2)
+        def dw_open(h, m0=0, m1=PACK):
+            for m in range(m0, m1):
+                dw_accs[m] = bank(m)
+                matmul(dw_accs[m], gated_q[0][h], m, g_tok_q[0], True, False)
 
-        def dw_open(gated_q, g_tok):
-            accs = [bank(m) for m in range(PACK)]
-            for m in range(PACK):
-                matmul(accs[m], gated_q, m, g_tok, True, False)
-            return accs
+        def dw_close(h, m0=0, m1=PACK):
+            for m in range(m0, m1):
+                matmul(dw_accs[m], gated_q[1][h], m, g_tok_q[1], False, True)
+                nc.scalar.copy(out=dw[h][:, m, :], in_=dw_accs[m][:])
 
-        def dw_close(h, accs, gated_q, g_tok):
-            for m in range(PACK):
-                matmul(accs[m], gated_q, m, g_tok, False, True)
-                nc.scalar.copy(out=dw[h][:, m, :], in_=accs[m][:])
+        def dw_store(h, m0=0, m1=PACK):
+            rows = out_1[half(h), :].rearrange("(m p) d -> p m d", p=P)
+            nc.sync.dma_start(out=rows[:, m0:m1, :], in_=dw[h][:, m0:m1, :])
 
-        def dw_store(h):
-            rows = out_1[h * HALF : (h + 1) * HALF, :].rearrange("(m p) d -> p m d", p=P)
-            for s in range(2):
-                nc.sync.dma_start(out=rows[:, 2 * s : 2 * s + 2, :], in_=dw[h][:, 2 * s : 2 * s + 2, :])
+        gated = [[sbuf("gated%d%d" % (b, h), [P, HALF * PACK], BF16) for h in range(2)] for b in range(B)]
+        du = [[sbuf("du%d%d" % (b, h), [P, PACK, HALF], F32) for h in range(2)] for b in range(B)]
+        dw = [sbuf("dw%d" % h, [P, PACK, D], F32) for h in range(2)]
+        g_feat_q = [mx_operand("g_feat%d" % b, E5M2) for b in range(B)]
+        g_tok_q = [mx_operand("g_tok%d" % b, E5M2) for b in range(B)]
+        w_q = [mx_operand("w%d" % h, E4M3) for h in range(2)]
+        gated_q = [[mx_operand("gated%d%d" % (b, h), E4M3) for h in range(2)] for b in range(B)]
 
-        g_tok0 = interleave_g(0, nc.vector.tensor_copy)
-        g_feat0 = transpose("g_feat0", g_raw[0], 0, True)
-        w_t0 = transpose("w_t0", w_raw[0], 2, False)
-        g_feat0_q = quantize("g_feat0", g_feat0, E5M2)
-        g_tok0_q = quantize("g_tok0", g_tok0, E5M2)
-        w_t1 = transpose("w_t1", w_raw[1], 0, False)
-        w_q = [quantize("w0", w_t0, E4M3), quantize("w1", w_t1, E4M3)]
+        g_raw, w_raw = {}, {}
+        u_raw, av_raw = [{}, {}], [{}, {}]
+        w_raw[0] = load_pairs("w_raw0", by_slot(W_o[half(0), :]), BF16)
+        g_raw[0] = load_pairs("g_raw0", by_slot(grad_out[0]), BF16)
+        av_raw[0][0] = load_pairs("av_raw00", by_slot(av[0])[:, :, half(0)], F32)
+        u_raw[0][0] = load("u_raw00", by_slot(u[0])[:, :, half(0)], BF16)
+        g_raw[1] = load("g_raw1", by_slot(grad_out[1]), BF16)
+        av_raw[1][0] = load("av_raw10", by_slot(av[1])[:, :, half(0)], F32)
+        u_raw[1][0] = load("u_raw10", by_slot(u[1])[:, :, half(0)], BF16)
+        w_raw[1] = load("w_raw1", by_slot(W_o[half(1), :]), BF16)
+        for b in range(B):
+            av_raw[b][1] = load("av_raw%d1" % b, by_slot(av[b])[:, :, half(1)], F32)
+            u_raw[b][1] = load("u_raw%d1" % b, by_slot(u[b])[:, :, half(1)], BF16)
+
+        ident = sbuf("ident", [P, P], F32)
+        make_identity(nc, ident[:])
+
+        w_t0 = transpose_w(0, 0)
+        g_feat0 = transpose_g(0, 2)
+        g_tok0 = interleave_g(0, nc.scalar.copy)
+        quantize(w_q[0], w_t0)
         for s in range(2):
-            du_pair(0, s, du_products(g_feat0_q, w_q, s))
+            quantize_pair(g_feat_q[0], g_feat0, s)
+            for j in range(2 * s, 2 * s + 2):
+                du_product(0, 0, j)
+        for j in range(PACK):
+            du_scale(0, 0, j)
+        du_store(0, 0)
 
-        g_feat1 = transpose("g_feat1", g_raw[1], 2, True)
+        g_feat1 = transpose_g(1, 0)
         g_tok1 = interleave_g(1, nc.scalar.copy)
-        gated0 = [gate(0, h) for h in range(2)]
-        g_feat1_q = quantize("g_feat1", g_feat1, E5M2)
-        gated0_q = [quantize("gated0%d" % h, gated0[h], E4M3) for h in range(2)]
-        g_tok1_q = quantize("g_tok1", g_tok1, E5M2)
-
-        accs = {}
-
-        def du_product(j, h):
-            acc = bank(DU_BANK + (2 * j + h) % 4)
-            matmul(acc, g_feat1_q, j, w_q[h], True, True)
-            accs[(j, h)] = acc
-
-        for j in range(2):
-            for h in range(2):
-                du_product(j, h)
-        dw_accs = dw_open(gated0_q[0], g_tok0_q)
-
-        gated10 = gate(1, 0)
-        du_scale(1, 0, 0, accs)
-        gated10_q = quantize("gated10", gated10, E4M3)
-        du_scale(1, 0, 1, accs)
-        du_store(1, 0, 1)
-        dw_close(0, dw_accs, gated10_q, g_tok1_q)
-        dw_store(0)
-        for h in range(2):
-            du_product(2, h)
-        dw_accs = dw_open(gated0_q[1], g_tok0_q)
-        gated11 = gate(1, 1)
-        du_scale(1, 1, 0, accs)
-        gated11_q = quantize("gated11", gated11, E4M3)
-        du_scale(1, 1, 1, accs)
-        du_store(1, 1, 2)
-        dw_close(1, dw_accs, gated11_q, g_tok1_q)
-        for h in range(2):
-            du_product(3, h)
-        for h in range(2):
-            du_scale(1, 2, h, accs)
-        du_store(1, 2, 3)
-        dw_store(1)
-        for h in range(2):
-            du_scale(1, 3, h, accs)
-        du_store(1, 3, 4)
+        gate(0, 0)
+        for s in range(2):
+            quantize_pair(g_feat_q[1], g_feat1, s)
+        for j in range(PACK):
+            du_product(1, 0, j)
+        quantize(gated_q[0][0], gated[0][0])
+        quantize(g_tok_q[0], g_tok0)
+        w_t1 = transpose_w(1, 0)
+        for j in range(PACK):
+            du_scale(1, 0, j)
+        du_store(1, 0)
+        dw_open(0)
+        gate(1, 0)
+        quantize(g_tok_q[1], g_tok1)
+        quantize(gated_q[1][0], gated[1][0])
+        dw_close(0)
+        dw_store(0, 0, 2)
+        dw_store(0, 2, 4)
+        quantize(w_q[1], w_t1)
+        for j in range(PACK):
+            du_product(0, 1, j)
+        gate(0, 1, 0, 256)
+        gate(1, 1, 0, 256)
+        quantize(gated_q[0][1], gated[0][1], 0, 256)
+        dw_open(1, 0, 2)
+        du_scale(0, 1, 0)
+        du_store(0, 1, 0, 1)
+        quantize(gated_q[1][1], gated[1][1], 0, 256)
+        dw_close(1, 0, 2)
+        du_product(1, 1, 0)
+        gate(0, 1, 256, 512)
+        dw_store(1, 0, 2)
+        gate(1, 1, 256, 512)
+        quantize(gated_q[0][1], gated[0][1], 256, 512)
+        dw_open(1, 2, 4)
+        du_scale(0, 1, 1)
+        du_store(0, 1, 1, 2)
+        quantize(gated_q[1][1], gated[1][1], 256, 512)
+        dw_close(1, 2, 4)
+        du_product(1, 1, 1)
+        for j in range(2, PACK):
+            du_scale(0, 1, j)
+            du_store(0, 1, j, j + 1)
+            du_product(1, 1, j)
+        dw_store(1, 2, 4)
+        for j in range(PACK):
+            du_scale(1, 1, j)
+            du_store(1, 1, j, j + 1)

@@ -16,6 +16,7 @@ P = 128
 PACK = 4
 HALF = 512
 RUN = 4
+GPSIMD_COLS = 192
 
 FLOPS = 2 * 2 * B * N * D * H
 BYTES = B * N * H * (2 + 4 + 4) + B * N * D * 2 + H * D * (2 + 4)
@@ -29,8 +30,8 @@ def tile_gatedattentionunit_pb_v_kernel(tc, q, k, u, v, W_o, b_o, av, grad_out, 
         ps = ctx.enter_context(tc.psum_pool(name="ps", bufs=1))
         ctx.enter_context(tc.manual_schedule())
 
-        def sbuf(name, shape, dtype):
-            return sb.tile(shape, dtype, name=name, align_bytes=64)
+        def sbuf(name, shape, dtype, tag=""):
+            return sb.tile(shape, dtype, name=name, tag=tag, align_bytes=64)
 
         def bank(index):
             return ps.tile([P, HALF], F32, name="bank%d" % index)
@@ -52,6 +53,9 @@ def tile_gatedattentionunit_pb_v_kernel(tc, q, k, u, v, W_o, b_o, av, grad_out, 
                 nc.sync.dma_start(out=tile[:, 2 * s : 2 * s + 2, :], in_=rows[:, 2 * s : 2 * s + 2, :])
             return tile
 
+        def load_av(b, s):
+            nc.sync.dma_start(out=av_raw[b][:, 2 * s : 2 * s + 2, :], in_=by_slot(av[b])[:, 2 * s : 2 * s + 2, :])
+
         def interleaved(view):
             return view.rearrange("p (c i t) -> p c t i", i=RUN, t=PACK)
 
@@ -68,7 +72,7 @@ def tile_gatedattentionunit_pb_v_kernel(tc, q, k, u, v, W_o, b_o, av, grad_out, 
             )
 
         def interleave_g(b, copy):
-            grouped = sbuf("g_tok%d" % b, [P, D * PACK], BF16)
+            grouped = sbuf("g_tok%d" % b, [P, D * PACK], BF16, "g_tok%d" % b)
             copy(out=interleaved(grouped[:]), in_=slot_runs(g_raw[b][:]))
             return grouped
 
@@ -120,125 +124,139 @@ def tile_gatedattentionunit_pb_v_kernel(tc, q, k, u, v, W_o, b_o, av, grad_out, 
             )
 
         def gate(b, h, c0=0, c1=HALF):
+            cols = slice(h * HALF + c0, h * HALF + c1)
             nc.vector.tensor_tensor(
                 out=interleaved(gated[b][h][:, PACK * c0 : PACK * c1]),
-                in0=slot_runs(u_raw[b][h][:, :, c0:c1]),
-                in1=slot_runs(av_raw[b][h][:, :, c0:c1]),
+                in0=slot_runs(u_raw[b][:, :, cols]),
+                in1=slot_runs(av_raw[b][:, :, cols]),
                 op=MULT,
             )
+
+        def gate_on_gpsimd(b, h, s, tag):
+            c0, c1 = GPSIMD_COLS * s, GPSIMD_COLS * (s + 1)
+            cols = slice(h * HALF + c0, h * HALF + c1)
+            rows = sbuf("gated_rows%d" % s, [P, PACK, GPSIMD_COLS], BF16, tag)
+            nc.gpsimd.tensor_tensor(out=rows[:], in0=u_raw[b][:, :, cols], in1=av_raw[b][:, :, cols], op=MULT)
+            nc.scalar.copy(out=interleaved(gated[b][h][:, PACK * c0 : PACK * c1]), in_=slot_runs(rows[:]))
 
         DU_BANK = 4
         du_accs = {}
         dw_accs = {}
 
         def du_product(b, h, j):
-            du_accs[j] = bank(DU_BANK + j)
-            matmul(du_accs[j], g_feat_q[b], j, w_q[h], True, True)
+            du_accs[j, h] = bank(DU_BANK + 2 * (j % 2) + h)
+            matmul(du_accs[j, h], g_feat_q[b], j, w_q[h], True, True)
 
         def du_scale(b, h, j):
-            nc.vector.tensor_tensor(out=du[b][h][:, j, :], in0=du_accs[j][:], in1=av_raw[b][h][:, j, :], op=MULT)
+            nc.vector.tensor_tensor(out=du[b][:, j, half(h)], in0=du_accs[j, h][:], in1=av_raw[b][:, j, half(h)], op=MULT)
 
-        def du_store(b, h, j0=0, j1=PACK):
-            nc.sync.dma_start(out=by_slot(out_0[b])[:, j0:j1, half(h)], in_=du[b][h][:, j0:j1, :])
+        def du_store(b, j0, j1):
+            nc.sync.dma_start(out=by_slot(out_0[b])[:, j0:j1, :], in_=du[b][:, j0:j1, :])
 
         def dw_open(h, m0=0, m1=PACK):
             for m in range(m0, m1):
-                dw_accs[m] = bank(m)
-                matmul(dw_accs[m], gated_q[0][h], m, g_tok_q[0], True, False)
+                dw_accs[h, m] = bank(PACK * h + m)
+                matmul(dw_accs[h, m], gated_q[0][h], m, g_tok_q[0], True, False)
 
         def dw_close(h, m0=0, m1=PACK):
             for m in range(m0, m1):
-                matmul(dw_accs[m], gated_q[1][h], m, g_tok_q[1], False, True)
-                nc.scalar.copy(out=dw[h][:, m, :], in_=dw_accs[m][:])
+                matmul(dw_accs[h, m], gated_q[1][h], m, g_tok_q[1], False, True)
+                nc.scalar.copy(out=dw[h][:, m, :], in_=dw_accs[h, m][:])
 
         def dw_store(h, m0=0, m1=PACK):
             rows = out_1[half(h), :].rearrange("(m p) d -> p m d", p=P)
             nc.sync.dma_start(out=rows[:, m0:m1, :], in_=dw[h][:, m0:m1, :])
 
-        gated = [[sbuf("gated%d%d" % (b, h), [P, HALF * PACK], BF16) for h in range(2)] for b in range(B)]
-        du = [[sbuf("du%d%d" % (b, h), [P, PACK, HALF], F32) for h in range(2)] for b in range(B)]
+        gated = [[sbuf("gated%d%d" % (b, h), [P, HALF * PACK], BF16, "gated%d%d" % (b, h)) for h in range(2)] for b in range(B)]
+        du = [sbuf("du%d" % b, [P, PACK, H], F32) for b in range(B)]
         dw = [sbuf("dw%d" % h, [P, PACK, D], F32) for h in range(2)]
         g_feat_q = [mx_operand("g_feat%d" % b, E5M2) for b in range(B)]
         g_tok_q = [mx_operand("g_tok%d" % b, E5M2) for b in range(B)]
         w_q = [mx_operand("w%d" % h, E4M3) for h in range(2)]
         gated_q = [[mx_operand("gated%d%d" % (b, h), E4M3) for h in range(2)] for b in range(B)]
 
-        g_raw, w_raw = {}, {}
-        u_raw, av_raw = [{}, {}], [{}, {}]
-        w_raw[0] = load_pairs("w_raw0", by_slot(W_o[half(0), :]), BF16)
+        g_raw, w_raw, u_raw = {}, {}, {}
+        av_raw = [sbuf("av_raw%d" % b, [P, PACK, H], F32) for b in range(B)]
         g_raw[0] = load_pairs("g_raw0", by_slot(grad_out[0]), BF16)
-        av_raw[0][0] = load_pairs("av_raw00", by_slot(av[0])[:, :, half(0)], F32)
-        u_raw[0][0] = load("u_raw00", by_slot(u[0])[:, :, half(0)], BF16)
-        g_raw[1] = load("g_raw1", by_slot(grad_out[1]), BF16)
-        av_raw[1][0] = load("av_raw10", by_slot(av[1])[:, :, half(0)], F32)
-        u_raw[1][0] = load("u_raw10", by_slot(u[1])[:, :, half(0)], BF16)
+        w_raw[0] = load_pairs("w_raw0", by_slot(W_o[half(0), :]), BF16)
         w_raw[1] = load("w_raw1", by_slot(W_o[half(1), :]), BF16)
-        for b in range(B):
-            av_raw[b][1] = load("av_raw%d1" % b, by_slot(av[b])[:, :, half(1)], F32)
-            u_raw[b][1] = load("u_raw%d1" % b, by_slot(u[b])[:, :, half(1)], BF16)
+        load_av(0, 0)
+        load_av(0, 1)
+        u_raw[0] = load("u_raw0", by_slot(u[0]), BF16)
+        g_raw[1] = load("g_raw1", by_slot(grad_out[1]), BF16)
+        load_av(1, 0)
+        u_raw[1] = load("u_raw1", by_slot(u[1]), BF16)
+        load_av(1, 1)
 
         ident = sbuf("ident", [P, P], F32)
         make_identity(nc, ident[:])
 
-        w_t0 = transpose_w(0, 0)
-        g_feat0 = transpose_g(0, 2)
-        g_tok0 = interleave_g(0, nc.scalar.copy)
-        quantize(w_q[0], w_t0)
+        g_feat0 = transpose_g(0, 0)
+        w_t0 = transpose_w(0, 2)
+        g_tok0 = interleave_g(0, nc.vector.tensor_copy)
         for s in range(2):
             quantize_pair(g_feat_q[0], g_feat0, s)
-            for j in range(2 * s, 2 * s + 2):
-                du_product(0, 0, j)
-        for j in range(PACK):
-            du_scale(0, 0, j)
-        du_store(0, 0)
+        quantize(g_tok_q[0], g_tok0)
+        quantize(w_q[0], w_t0)
+        w_t1 = transpose_w(1, 0)
+        for j in range(2):
+            du_product(0, 0, j)
+        quantize(w_q[1], w_t1)
+        for j in range(2):
+            du_product(0, 1, j)
+        for h in range(2):
+            for j in range(2):
+                du_scale(0, h, j)
+                du_product(0, h, j + 2)
+        du_store(0, 0, 2)
+        for h in range(2):
+            for j in range(2, PACK):
+                du_scale(0, h, j)
+        du_store(0, 2, PACK)
 
         g_feat1 = transpose_g(1, 0)
         g_tok1 = interleave_g(1, nc.scalar.copy)
         gate(0, 0)
+        gate(0, 1, 2 * GPSIMD_COLS, HALF)
         for s in range(2):
             quantize_pair(g_feat_q[1], g_feat1, s)
-        for j in range(PACK):
-            du_product(1, 0, j)
+        for j in range(2):
+            for h in range(2):
+                du_product(1, h, j)
         quantize(gated_q[0][0], gated[0][0])
-        quantize(g_tok_q[0], g_tok0)
-        w_t1 = transpose_w(1, 0)
-        for j in range(PACK):
-            du_scale(1, 0, j)
-        du_store(1, 0)
+        gate_on_gpsimd(0, 1, 0, "gated00")
+        for j in range(2):
+            for h in range(2):
+                du_scale(1, h, j)
+                du_product(1, h, j + 2)
+        du_store(1, 0, 2)
         dw_open(0)
-        gate(1, 0)
         quantize(g_tok_q[1], g_tok1)
-        quantize(gated_q[1][0], gated[1][0])
-        dw_close(0)
-        dw_store(0, 0, 2)
-        dw_store(0, 2, 4)
-        quantize(w_q[1], w_t1)
-        for j in range(PACK):
-            du_product(0, 1, j)
-        gate(0, 1, 0, 256)
-        gate(1, 1, 0, 256)
-        quantize(gated_q[0][1], gated[0][1], 0, 256)
-        dw_open(1, 0, 2)
-        du_scale(0, 1, 0)
-        du_store(0, 1, 0, 1)
-        quantize(gated_q[1][1], gated[1][1], 0, 256)
-        dw_close(1, 0, 2)
-        du_product(1, 1, 0)
-        gate(0, 1, 256, 512)
-        dw_store(1, 0, 2)
-        gate(1, 1, 256, 512)
-        quantize(gated_q[0][1], gated[0][1], 256, 512)
-        dw_open(1, 2, 4)
-        du_scale(0, 1, 1)
-        du_store(0, 1, 1, 2)
-        quantize(gated_q[1][1], gated[1][1], 256, 512)
-        dw_close(1, 2, 4)
-        du_product(1, 1, 1)
+        gate_on_gpsimd(0, 1, 1, "g_tok1")
         for j in range(2, PACK):
-            du_scale(0, 1, j)
-            du_store(0, 1, j, j + 1)
-            du_product(1, 1, j)
-        dw_store(1, 2, 4)
-        for j in range(PACK):
-            du_scale(1, 1, j)
-            du_store(1, 1, j, j + 1)
+            for h in range(2):
+                du_scale(1, h, j)
+        du_store(1, 2, PACK)
+
+        def open_pair(s):
+            quantize(gated_q[0][1], gated[0][1], 2 * P * s, 2 * P * (s + 1))
+            dw_open(1, 2 * s, 2 * s + 2)
+
+        def finish(h, m0, m1):
+            quantize(gated_q[1][h], gated[1][h], P * m0, P * m1)
+            for m in range(m0, m1):
+                dw_close(h, m, m + 1)
+                dw_store(h, m, m + 1)
+
+        gate(1, 0, 0, 2 * P)
+        open_pair(0)
+        gate(1, 0, 2 * P, 4 * P)
+        finish(0, 0, 2)
+        open_pair(1)
+        finish(0, 2, 4)
+        gate(1, 1, 0, 2 * P)
+        gate(1, 1, 2 * P, 3 * P)
+        finish(1, 0, 2)
+        gate(1, 1, 3 * P, 4 * P)
+        finish(1, 2, 3)
+        finish(1, 3, 4)

from contextlib import ExitStack

import concourse.mybir as mybir
from concourse.masks import make_identity

F32 = mybir.dt.float32
BF16 = mybir.dt.bfloat16
U32 = mybir.dt.uint32
U8 = mybir.dt.uint8
E4M3 = mybir.dt.float8_e4m3fn_x4
E5M2 = mybir.dt.float8_e5m2_x4
MULT = mybir.AluOpType.mult

B, N, D, H = 2, 512, 512, 1024
P = 128
PACK = 4
HALF = 512
RUN = 4
GPSIMD_COLS = 192

FLOPS = 2 * 2 * B * N * D * H
BYTES = B * N * H * (2 + 4 + 4) + B * N * D * 2 + H * D * (2 + 4)


def tile_gatedattentionunit_pb_v_kernel(tc, q, k, u, v, W_o, b_o, av, grad_out, out_0, out_1):
    nc = tc.nc

    with ExitStack() as ctx:
        sb = ctx.enter_context(tc.tile_pool(name="sb", bufs=1))
        ps = ctx.enter_context(tc.psum_pool(name="ps", bufs=1))
        ctx.enter_context(tc.manual_schedule())

        def sbuf(name, shape, dtype, tag=""):
            return sb.tile(shape, dtype, name=name, tag=tag, align_bytes=64)

        def bank(index):
            return ps.tile([P, HALF], F32, name="bank%d" % index)

        def by_slot(rows):
            return rows.rearrange("(p j) w -> p j w", j=PACK)

        def half(h):
            return slice(h * HALF, (h + 1) * HALF)

        def load(name, rows, dtype):
            tile = sbuf(name, list(rows.shape), dtype)
            nc.sync.dma_start(out=tile[:], in_=rows)
            return tile

        def load_pairs(name, rows, dtype):
            tile = sbuf(name, list(rows.shape), dtype)
            for s in range(2):
                nc.sync.dma_start(out=tile[:, 2 * s : 2 * s + 2, :], in_=rows[:, 2 * s : 2 * s + 2, :])
            return tile

        def load_av(b, s):
            nc.sync.dma_start(out=av_raw[b][:, 2 * s : 2 * s + 2, :], in_=by_slot(av[b])[:, 2 * s : 2 * s + 2, :])

        def interleaved(view):
            return view.rearrange("p (c i t) -> p c t i", i=RUN, t=PACK)

        def slot_runs(view):
            return view.rearrange("p t (c i) -> p c t i", i=RUN)

        def mx_operand(name, fmt):
            return sbuf(name + "_codes", [P, HALF], U32), sbuf(name + "_scales", [P, HALF], U8), fmt

        def quantize(operand, grouped, c0=0, c1=HALF):
            codes, scales, fmt = operand
            nc.vector.quantize_mx(
                out=codes[:, c0:c1].bitcast(fmt), scales=scales[:, c0:c1], in_=grouped[:, PACK * c0 : PACK * c1]
            )

        def interleave_g(b, copy):
            grouped = sbuf("g_tok%d" % b, [P, D * PACK], BF16, "g_tok%d" % b)
            copy(out=interleaved(grouped[:]), in_=slot_runs(g_raw[b][:]))
            return grouped

        def transpose_pair(raw, s, bank_index):
            xt = bank(bank_index)
            for jj in range(2):
                words = raw[:, 2 * s + jj, :].bitcast(F32)
                for e in range(2):
                    nc.tensor.transpose(xt[:, (2 * jj + e) * P : (2 * jj + e + 1) * P], words[:, e::2], ident[:])
            return xt

        def transpose_g(b, first_bank):
            tiles = []
            for s in range(2):
                xt = transpose_pair(g_raw[b], s, first_bank + s)
                grouped = sbuf("g_feat%d%d" % (b, s), [P, 2 * P * PACK], BF16)
                nc.scalar.copy(
                    out=grouped[:].bitcast(F32).rearrange("p (j r e) -> p j r e", j=2, e=2),
                    in_=xt[:].rearrange("p (j e r) -> p j r e", j=2, e=2),
                )
                tiles.append(grouped)
            return tiles

        def quantize_pair(operand, grouped, s):
            codes, scales, fmt = operand
            cols = slice(2 * P * s, 2 * P * (s + 1))
            nc.vector.quantize_mx(out=codes[:, cols].bitcast(fmt), scales=scales[:, cols], in_=grouped[s][:])

        def transpose_w(h, first_bank):
            grouped = sbuf("w_t%d" % h, [P, HALF * PACK], BF16)
            for s in range(2):
                xt = transpose_pair(w_raw[h], s, first_bank + s)
                nc.scalar.copy(
                    out=grouped[:].bitcast(F32).rearrange("p (r j e) -> p r j e", j=PACK, e=2)[:, :, 2 * s : 2 * s + 2, :],
                    in_=xt[:].rearrange("p (j e r) -> p r j e", j=2, e=2),
                )
            return grouped

        def matmul(acc, stationary, block, moving, start, stop):
            cols = slice(block * P, (block + 1) * P)
            nc.tensor.matmul_mx(
                out=acc[:],
                lhsT=stationary[0][:, cols].bitcast(stationary[2]),
                lhsT_scale=stationary[1][:, cols],
                rhs=moving[0][:].bitcast(moving[2]),
                rhs_scale=moving[1][:],
                start=start,
                stop=stop,
            )

        def gate(b, h, c0=0, c1=HALF):
            cols = slice(h * HALF + c0, h * HALF + c1)
            nc.vector.tensor_tensor(
                out=interleaved(gated[b][h][:, PACK * c0 : PACK * c1]),
                in0=slot_runs(u_raw[b][:, :, cols]),
                in1=slot_runs(av_raw[b][:, :, cols]),
                op=MULT,
            )

        def gate_on_gpsimd(b, h, s, tag):
            c0, c1 = GPSIMD_COLS * s, GPSIMD_COLS * (s + 1)
            cols = slice(h * HALF + c0, h * HALF + c1)
            rows = sbuf("gated_rows%d" % s, [P, PACK, GPSIMD_COLS], BF16, tag)
            nc.gpsimd.tensor_tensor(out=rows[:], in0=u_raw[b][:, :, cols], in1=av_raw[b][:, :, cols], op=MULT)
            nc.scalar.copy(out=interleaved(gated[b][h][:, PACK * c0 : PACK * c1]), in_=slot_runs(rows[:]))

        DU_BANK = 4
        du_accs = {}
        dw_accs = {}

        def du_product(b, h, j):
            du_accs[j, h] = bank(DU_BANK + 2 * (j % 2) + h)
            matmul(du_accs[j, h], g_feat_q[b], j, w_q[h], True, True)

        def du_scale(b, h, j):
            nc.vector.tensor_tensor(out=du[b][:, j, half(h)], in0=du_accs[j, h][:], in1=av_raw[b][:, j, half(h)], op=MULT)

        def du_store(b, j0, j1):
            nc.sync.dma_start(out=by_slot(out_0[b])[:, j0:j1, :], in_=du[b][:, j0:j1, :])

        def dw_open(h, m0=0, m1=PACK):
            for m in range(m0, m1):
                dw_accs[h, m] = bank(PACK * h + m)
                matmul(dw_accs[h, m], gated_q[0][h], m, g_tok_q[0], True, False)

        def dw_close(h, m0=0, m1=PACK):
            for m in range(m0, m1):
                matmul(dw_accs[h, m], gated_q[1][h], m, g_tok_q[1], False, True)
                nc.scalar.copy(out=dw[h][:, m, :], in_=dw_accs[h, m][:])

        def dw_store(h, m0=0, m1=PACK):
            rows = out_1[half(h), :].rearrange("(m p) d -> p m d", p=P)
            nc.sync.dma_start(out=rows[:, m0:m1, :], in_=dw[h][:, m0:m1, :])

        gated = [[sbuf("gated%d%d" % (b, h), [P, HALF * PACK], BF16, "gated%d%d" % (b, h)) for h in range(2)] for b in range(B)]
        du = [sbuf("du%d" % b, [P, PACK, H], F32) for b in range(B)]
        dw = [sbuf("dw%d" % h, [P, PACK, D], F32) for h in range(2)]
        g_feat_q = [mx_operand("g_feat%d" % b, E5M2) for b in range(B)]
        g_tok_q = [mx_operand("g_tok%d" % b, E5M2) for b in range(B)]
        w_q = [mx_operand("w%d" % h, E4M3) for h in range(2)]
        gated_q = [[mx_operand("gated%d%d" % (b, h), E4M3) for h in range(2)] for b in range(B)]

        g_raw, w_raw, u_raw = {}, {}, {}
        av_raw = [sbuf("av_raw%d" % b, [P, PACK, H], F32) for b in range(B)]
        g_raw[0] = load_pairs("g_raw0", by_slot(grad_out[0]), BF16)
        w_raw[0] = load_pairs("w_raw0", by_slot(W_o[half(0), :]), BF16)
        w_raw[1] = load("w_raw1", by_slot(W_o[half(1), :]), BF16)
        load_av(0, 0)
        load_av(0, 1)
        u_raw[0] = load("u_raw0", by_slot(u[0]), BF16)
        g_raw[1] = load("g_raw1", by_slot(grad_out[1]), BF16)
        load_av(1, 0)
        u_raw[1] = load("u_raw1", by_slot(u[1]), BF16)
        load_av(1, 1)

        ident = sbuf("ident", [P, P], F32)
        make_identity(nc, ident[:])

        g_feat0 = transpose_g(0, 0)
        w_t0 = transpose_w(0, 2)
        g_tok0 = interleave_g(0, nc.vector.tensor_copy)
        for s in range(2):
            quantize_pair(g_feat_q[0], g_feat0, s)
        quantize(g_tok_q[0], g_tok0)
        quantize(w_q[0], w_t0)
        w_t1 = transpose_w(1, 0)
        for j in range(2):
            du_product(0, 0, j)
        quantize(w_q[1], w_t1)
        for j in range(2):
            du_product(0, 1, j)
        for h in range(2):
            for j in range(2):
                du_scale(0, h, j)
                du_product(0, h, j + 2)
        du_store(0, 0, 2)
        for h in range(2):
            for j in range(2, PACK):
                du_scale(0, h, j)
        du_store(0, 2, PACK)

        g_feat1 = transpose_g(1, 0)
        g_tok1 = interleave_g(1, nc.scalar.copy)
        gate(0, 0)
        gate(0, 1, 2 * GPSIMD_COLS, HALF)
        for s in range(2):
            quantize_pair(g_feat_q[1], g_feat1, s)
        for j in range(2):
            for h in range(2):
                du_product(1, h, j)
        quantize(gated_q[0][0], gated[0][0])
        gate_on_gpsimd(0, 1, 0, "gated00")
        for j in range(2):
            for h in range(2):
                du_scale(1, h, j)
                du_product(1, h, j + 2)
        du_store(1, 0, 2)
        dw_open(0)
        quantize(g_tok_q[1], g_tok1)
        gate_on_gpsimd(0, 1, 1, "g_tok1")
        for j in range(2, PACK):
            for h in range(2):
                du_scale(1, h, j)
        du_store(1, 2, PACK)

        def open_pair(s):
            quantize(gated_q[0][1], gated[0][1], 2 * P * s, 2 * P * (s + 1))
            dw_open(1, 2 * s, 2 * s + 2)

        def finish(h, m0, m1):
            quantize(gated_q[1][h], gated[1][h], P * m0, P * m1)
            for m in range(m0, m1):
                dw_close(h, m, m + 1)
                dw_store(h, m, m + 1)

        gate(1, 0, 0, 2 * P)
        open_pair(0)
        gate(1, 0, 2 * P, 4 * P)
        finish(0, 0, 2)
        open_pair(1)
        finish(0, 2, 4)
        gate(1, 1, 0, 2 * P)
        gate(1, 1, 2 * P, 3 * P)
        finish(1, 0, 2)
        gate(1, 1, 3 * P, 4 * P)
        finish(1, 2, 3)
        finish(1, 3, 4)
